import numpy as np
import ml_dtypes


def mxq(x, axis, fmt="e4m3"):
    dtype, down = {"e4m3": (ml_dtypes.float8_e4m3fn, 7), "e5m2": (ml_dtypes.float8_e5m2, 14)}[fmt]
    v = np.moveaxis(np.asarray(x, np.float32).astype(ml_dtypes.bfloat16).astype(np.float64), axis, -1)
    blocks = v.reshape(v.shape[:-1] + (-1, 32))
    amax = np.abs(blocks).max(-1, keepdims=True)
    byte = np.maximum(np.where(amax > 0, np.frexp(amax)[1] - 1 + 127, 0) - down, 1)
    scale = np.exp2(byte - 127.0)
    codes = (blocks / scale).astype(np.float32).astype(dtype).astype(np.float64)
    return np.moveaxis((codes * scale).reshape(v.shape), -1, axis)


WIDE = False


def mx_kscale(k):
    if not WIDE:
        return np.ones(k)
    levels = np.array([10, -10, 5, -5, 0])
    a = np.random.permutation(np.resize(levels, k // 512 * 4)).reshape(k // 512, 4)
    idx = np.arange(k)
    return np.exp2(a[idx // 512, idx % 128 // 32])


BF16 = ml_dtypes.bfloat16


def bf(x):
    return np.asarray(x, np.float32).astype(BF16)


def f64(x):
    return np.asarray(x).astype(np.float64)


S, B, SC = 4096, 1024, 1024


def setup_inputs():
    s = mx_kscale(B)
    return {"proba": bf((np.random.standard_normal((S, B)) * s).reshape(-1)),
            "cur_inven": bf(np.random.random_sample((S, SC))),
            "bun_sc": bf(np.random.random_sample((B, SC)) * (16.0 / np.sqrt(B)) / s[:, None]),
            "avail_bundle": bf(np.random.random_sample(B) * s),
            "alloc_bundle": bf(np.random.random_sample(B) * s)}


def reference(proba, cur_inven, bun_sc, avail_bundle, alloc_bundle):
    p = f64(proba).reshape(S, B)
    av = f64(avail_bundle)
    al = f64(alloc_bundle)
    over_avail = (av[None, :] - p < 0.0) & (p > 0.0)
    over_alloc = (al[None, :] + p < 0.0) & (p < 0.0)
    cm = np.where(over_avail | over_alloc, 0.01, 1.0)
    next_inven = f64(cur_inven) + (mxq(p * cm, 1, "e4m3") @ mxq(f64(bun_sc), 0, "e4m3"))
    return next_inven.reshape(1, -1)

@@ -1,0 +1,229 @@
+from contextlib import ExitStack
+
+import concourse.mybir as mybir
+from concourse.masks import make_identity
+
+FP8X4 = mybir.dt.float8_e4m3fn_x4
+BF16 = mybir.dt.bfloat16
+F32 = mybir.dt.float32
+U32 = mybir.dt.uint32
+U8 = mybir.dt.uint8
+ALU = mybir.AluOpType
+
+S, B, SC = 4096, 1024, 1024
+FLOPS = 2 * S * B * SC
+
+P = 128
+JT = 4
+ROWS = P * JT
+NST = S // ROWS
+G = B // 512
+PIN = False
+DVE_BANKS = ()
+
+
+def tile_optblockv2_t_kernel(tc, proba, cur_inven, bun_sc, avail_bundle, alloc_bundle, out):
+    nc = tc.nc
+    xv = proba.rearrange("(i r q) -> i r q", r=P, q=JT * B)
+    cv = cur_inven.rearrange("(i r j) n -> i r (j n)", r=P, j=JT)
+    ov = out.rearrange("o (i r q) -> (o i) r q", r=P, q=JT * SC)
+    bv = bun_sc.rearrange("(g t p) n -> g p t n", t=4, p=P)
+
+    with ExitStack() as ctx:
+        const = ctx.enter_context(tc.tile_pool(name="const", bufs=1))
+        xin = ctx.enter_context(tc.tile_pool(name="xin", bufs=3))
+        cin = ctx.enter_context(tc.tile_pool(name="cin", bufs=4))
+        oout = ctx.enter_context(tc.tile_pool(name="oout", bufs=3))
+        work = ctx.enter_context(tc.tile_pool(name="work", bufs=2))
+        xtp = ctx.enter_context(tc.psum_pool(name="xtp", bufs=4))
+        accp = ctx.enter_context(tc.psum_pool(name="accp", bufs=4))
+        if PIN:
+            ctx.enter_context(tc.manual_schedule())
+
+        ident = const.tile([P, P], BF16)
+        make_identity(nc, ident[:])
+        vt = const.tile([P, P], BF16)
+        nc.vector.memset(vt[:], 0.0)
+        nc.sync.dma_start(out=vt[0:8, :], in_=avail_bundle.rearrange("(c p) -> c p", p=P))
+        nc.sync.dma_start(out=vt[8:16, :], in_=alloc_bundle.rearrange("(c p) -> c p", p=P))
+
+        braw = const.tile([P, 2 * 4, SC], BF16)
+        x_t = {}
+        c_t = {}
+        o_t = {}
+
+        def load_b(g):
+            nc.sync.dma_start(out=braw[:, 4 * g : 4 * g + 4, :], in_=bv[g])
+
+        def load_x(i):
+            xt = xin.tile([P, JT, B], BF16, name="xt")
+            nc.sync.dma_start(out=xt[:].rearrange("p j k -> p (j k)"), in_=xv[i])
+            x_t[i] = xt
+
+        def load_c(i):
+            ct = cin.tile([P, JT, SC], BF16, name="ct")
+            nc.sync.dma_start(out=ct[:].rearrange("p j n -> p (j n)"), in_=cv[i])
+            c_t[i] = ct
+
+        load_b(0)
+        load_x(0)
+        load_b(1)
+        load_c(0)
+        load_x(1)
+        load_c(1)
+
+        thr_ps = xtp.tile([P, P], BF16, tag="xt", name="thr_ps")
+        nc.tensor.transpose(thr_ps[:], vt[:], ident[:])
+        thr = const.tile([P, 16], F32)
+        nc.vector.tensor_scalar(out=thr[:, 0:8], in0=thr_ps[:, 0:8], scalar1=0.0, scalar2=None, op0=ALU.max)
+        nc.vector.tensor_scalar(
+            out=thr[:, 8:16], in0=thr_ps[:, 8:16], scalar1=-1.0, scalar2=0.0, op0=ALU.mult, op1=ALU.min
+        )
+
+        bcodes = const.tile([P, G, SC], U32, align_bytes=64)
+        bscl = const.tile([P, G, SC], U8, align_bytes=64)
+        bgrp = {}
+
+        def regroup_b(g, eng):
+            bg = const.tile([P, SC, 4], BF16, align_bytes=64, name="bgrp%d" % g)
+            dst = bg[:].rearrange("p (c i) t -> p c t i", i=4)
+            src = braw[:, 4 * g : 4 * g + 4, :].rearrange("p t (c i) -> p c t i", i=4)
+            if eng == "v":
+                nc.vector.tensor_copy(out=dst, in_=src)
+            else:
+                nc.scalar.copy(out=dst, in_=src)
+            bgrp[g] = bg
+
+        def quant_b(g):
+            nc.vector.quantize_mx(
+                out=bcodes[:, g, :].bitcast(FP8X4),
+                scales=bscl[:, g, :],
+                in_=bgrp[g][:].rearrange("p n t -> p (n t)"),
+            )
+
+        banks = {}
+        xs_t = {}
+        codes_t = {}
+        scl_t = {}
+
+        def transposes(i, g):
+            for b in range(2):
+                bank = xtp.tile([P, 4, 256], BF16, tag="xt", name="bank")
+                for t in range(4):
+                    for jj in range(2):
+                        k0 = 512 * g + 128 * t
+                        nc.tensor.transpose(
+                            bank[:, t, 128 * jj : 128 * jj + 128], x_t[i][:, 2 * b + jj, k0 : k0 + 128], ident[:]
+                        )
+                banks[(i, g, b)] = bank
+
+        def copies(i, g):
+            xs = work.tile([P, 4, ROWS], BF16, name="xs", bufs=3)
+            for b in range(2):
+                nc.scalar.copy(out=xs[:, :, 256 * b : 256 * b + 256], in_=banks[(i, g, b)][:])
+            xs_t[(i, g)] = xs
+
+        def masks(i, g):
+            if g == 0:
+                codes = work.tile([P, G, ROWS], U32, align_bytes=64, name="codes")
+                scl = work.tile([P, G, ROWS], U8, align_bytes=64, name="scl")
+                codes_t[i] = codes
+                scl_t[i] = scl
+            xs = xs_t[(i, g)]
+            cl = work.tile([P, 4, ROWS], BF16, name="cl")
+            kp = work.tile([P, 4, ROWS], BF16, name="kp")
+            h = work.tile([P, ROWS, 4], BF16, align_bytes=64, name="h")
+            for t in range(4):
+                ch = 4 * g + t
+                nc.vector.tensor_scalar(
+                    out=cl[:, t, :],
+                    in0=xs[:, t, :],
+                    scalar1=thr[:, 8 + ch : 9 + ch],
+                    scalar2=thr[:, ch : ch + 1],
+                    op0=ALU.max,
+                    op1=ALU.min,
+                )
+            for b in range(2):
+                cols = slice(256 * b, 256 * b + 256)
+                bank = banks[(i, g, b)]
+                nc.vector.tensor_tensor(out=kp[:, :, cols], in0=cl[:, :, cols], in1=bank[:], op=ALU.is_equal)
+            for b in range(2):
+                cols = slice(256 * b, 256 * b + 256)
+                bank = banks[(i, g, b)]
+                nc.vector.scalar_tensor_tensor(
+                    out=h[:, cols, :],
+                    in0=kp[:, :, cols].rearrange("p t s -> p s t"),
+                    scalar=0.01,
+                    in1=bank[:].rearrange("p t s -> p s t"),
+                    op0=ALU.max,
+                    op1=ALU.mult,
+                )
+            nc.vector.quantize_mx(
+                out=codes_t[i][:, g, :].bitcast(FP8X4),
+                scales=scl_t[i][:, g, :],
+                in_=h[:].rearrange("p s t -> p (s t)"),
+            )
+
+        def matmuls(i):
+            ot = oout.tile([P, JT, SC], F32, name="ot")
+            o_t[i] = ot
+            codes = codes_t[i]
+            scl = scl_t[i]
+            ct = c_t[i]
+            for j in range(JT):
+                act_cols = []
+                for hf in range(2):
+                    acc = accp.tile([P, 512], F32, name="acc")
+                    for g in range(G):
+                        nc.tensor.matmul_mx(
+                            out=acc[:],
+                            lhsT=codes[:, g, 128 * j : 128 * j + 128].bitcast(FP8X4),
+                            lhsT_scale=scl[:, g, 128 * j : 128 * j + 128],
+                            rhs=bcodes[:, g, 512 * hf : 512 * hf + 512].bitcast(FP8X4),
+                            rhs_scale=bscl[:, g, 512 * hf : 512 * hf + 512],
+                            start=(g == 0),
+                            stop=(g == G - 1),
+                        )
+                    cols = slice(512 * hf, 512 * hf + 512)
+                    if (j, hf) in DVE_BANKS or i == NST - 1:
+                        nc.vector.tensor_tensor(out=ot[:, j, cols], in0=acc[:], in1=ct[:, j, cols], op=ALU.add)
+                    else:
+                        nc.scalar.copy(out=ot[:, j, cols], in_=acc[:])
+                        act_cols.append(hf)
+                if len(act_cols) == 2:
+                    nc.gpsimd.tensor_tensor(out=ot[:, j, :], in0=ot[:, j, :], in1=ct[:, j, :], op=ALU.add)
+                elif len(act_cols) == 1:
+                    cols = slice(512 * act_cols[0], 512 * act_cols[0] + 512)
+                    nc.gpsimd.tensor_tensor(out=ot[:, j, cols], in0=ot[:, j, cols], in1=ct[:, j, cols], op=ALU.add)
+                if i == NST - 1:
+                    nc.sync.dma_start(out=ov[i][:, SC * j : SC * j + SC], in_=ot[:, j, :])
+
+        def store(i):
+            if i < NST - 1:
+                nc.sync.dma_start(out=ov[i], in_=o_t[i][:].rearrange("p j n -> p (j n)"))
+
+        regroup_b(0, "v")
+        quant_b(0)
+        transposes(0, 0)
+        copies(0, 0)
+        transposes(0, 1)
+        copies(0, 1)
+        regroup_b(1, "s")
+        masks(0, 0)
+        quant_b(1)
+        masks(0, 1)
+
+        for i in range(NST):
+            if i + 2 < NST:
+                load_x(i + 2)
+                load_c(i + 2)
+            if i + 1 < NST:
+                transposes(i + 1, 0)
+                copies(i + 1, 0)
+                transposes(i + 1, 1)
+                copies(i + 1, 1)
+            matmuls(i)
+            if i + 1 < NST:
+                masks(i + 1, 0)
+                masks(i + 1, 1)
+            store(i)

@@ -18,8 +18,9 @@ JT = 4
 ROWS = P * JT
 NST = S // ROWS
 G = B // 512
-PIN = False
-DVE_BANKS = ()
+NU = NST * G
+PIN = True
+DVE_BANKS = (3, 7)
 
 
 def tile_optblockv2_t_kernel(tc, proba, cur_inven, bun_sc, avail_bundle, alloc_bundle, out):
@@ -40,24 +41,36 @@ def tile_optblockv2_t_kernel(tc, proba, cur_inven, bun_sc, avail_bundle, alloc_b
         if PIN:
             ctx.enter_context(tc.manual_schedule())
 
+        x_t = {}
+        c_t = {}
+        o_t = {}
+        banks = {}
+        xs_t = {}
+        cl_t = {}
+        h_t = {}
+        codes_t = {}
+        scl_t = {}
+        bgrp = {}
+        pend = {}
+
         ident = const.tile([P, P], BF16)
         make_identity(nc, ident[:])
         vt = const.tile([P, P], BF16)
         nc.vector.memset(vt[:], 0.0)
-        nc.sync.dma_start(out=vt[0:8, :], in_=avail_bundle.rearrange("(c p) -> c p", p=P))
-        nc.sync.dma_start(out=vt[8:16, :], in_=alloc_bundle.rearrange("(c p) -> c p", p=P))
-
         braw = const.tile([P, 2 * 4, SC], BF16)
-        x_t = {}
-        c_t = {}
-        o_t = {}
+        bcodes = const.tile([P, G, SC], U32, align_bytes=64)
+        bscl = const.tile([P, G, SC], U8, align_bytes=64)
+        thr = const.tile([P, 16], F32)
 
         def load_b(g):
             nc.sync.dma_start(out=braw[:, 4 * g : 4 * g + 4, :], in_=bv[g])
 
-        def load_x(i):
+        def load_x(i, pieces=1):
             xt = xin.tile([P, JT, B], BF16, name="xt")
-            nc.sync.dma_start(out=xt[:].rearrange("p j k -> p (j k)"), in_=xv[i])
+            w = JT * B // pieces
+            flat = xt[:].rearrange("p j k -> p (j k)")
+            for q in range(pieces):
+                nc.sync.dma_start(out=flat[:, w * q : w * q + w], in_=xv[i][:, w * q : w * q + w])
             x_t[i] = xt
 
         def load_c(i):
@@ -65,33 +78,16 @@ def tile_optblockv2_t_kernel(tc, proba, cur_inven, bun_sc, avail_bundle, alloc_b
             nc.sync.dma_start(out=ct[:].rearrange("p j n -> p (j n)"), in_=cv[i])
             c_t[i] = ct
 
-        load_b(0)
-        load_x(0)
-        load_b(1)
-        load_c(0)
-        load_x(1)
-        load_c(1)
-
-        thr_ps = xtp.tile([P, P], BF16, tag="xt", name="thr_ps")
-        nc.tensor.transpose(thr_ps[:], vt[:], ident[:])
-        thr = const.tile([P, 16], F32)
-        nc.vector.tensor_scalar(out=thr[:, 0:8], in0=thr_ps[:, 0:8], scalar1=0.0, scalar2=None, op0=ALU.max)
-        nc.vector.tensor_scalar(
-            out=thr[:, 8:16], in0=thr_ps[:, 8:16], scalar1=-1.0, scalar2=0.0, op0=ALU.mult, op1=ALU.min
-        )
-
-        bcodes = const.tile([P, G, SC], U32, align_bytes=64)
-        bscl = const.tile([P, G, SC], U8, align_bytes=64)
-        bgrp = {}
-
         def regroup_b(g, eng):
             bg = const.tile([P, SC, 4], BF16, align_bytes=64, name="bgrp%d" % g)
             dst = bg[:].rearrange("p (c i) t -> p c t i", i=4)
             src = braw[:, 4 * g : 4 * g + 4, :].rearrange("p t (c i) -> p c t i", i=4)
             if eng == "v":
                 nc.vector.tensor_copy(out=dst, in_=src)
-            else:
+            elif eng == "s":
                 nc.scalar.copy(out=dst, in_=src)
+            else:
+                nc.gpsimd.tensor_scalar(out=dst, in0=src, scalar1=1.0, scalar2=0.0, op0=ALU.mult, op1=ALU.add)
             bgrp[g] = bg
 
         def quant_b(g):
@@ -101,12 +97,8 @@ def tile_optblockv2_t_kernel(tc, proba, cur_inven, bun_sc, avail_bundle, alloc_b
                 in_=bgrp[g][:].rearrange("p n t -> p (n t)"),
             )
 
-        banks = {}
-        xs_t = {}
-        codes_t = {}
-        scl_t = {}
-
-        def transposes(i, g):
+        def transposes(v):
+            i, g = divmod(v, G)
             for b in range(2):
                 bank = xtp.tile([P, 4, 256], BF16, tag="xt", name="bank")
                 for t in range(4):
@@ -115,115 +107,151 @@ def tile_optblockv2_t_kernel(tc, proba, cur_inven, bun_sc, avail_bundle, alloc_b
                         nc.tensor.transpose(
                             bank[:, t, 128 * jj : 128 * jj + 128], x_t[i][:, 2 * b + jj, k0 : k0 + 128], ident[:]
                         )
-                banks[(i, g, b)] = bank
+                banks[(v, b)] = bank
 
-        def copies(i, g):
+        def copies(v):
             xs = work.tile([P, 4, ROWS], BF16, name="xs", bufs=3)
             for b in range(2):
-                nc.scalar.copy(out=xs[:, :, 256 * b : 256 * b + 256], in_=banks[(i, g, b)][:])
-            xs_t[(i, g)] = xs
+                nc.scalar.copy(out=xs[:, :, 256 * b : 256 * b + 256], in_=banks[(v, b)][:])
+            xs_t[v] = xs
 
-        def masks(i, g):
-            if g == 0:
-                codes = work.tile([P, G, ROWS], U32, align_bytes=64, name="codes")
-                scl = work.tile([P, G, ROWS], U8, align_bytes=64, name="scl")
-                codes_t[i] = codes
-                scl_t[i] = scl
-            xs = xs_t[(i, g)]
+        def clamps(v):
+            g = v % G
             cl = work.tile([P, 4, ROWS], BF16, name="cl")
-            kp = work.tile([P, 4, ROWS], BF16, name="kp")
-            h = work.tile([P, ROWS, 4], BF16, align_bytes=64, name="h")
             for t in range(4):
                 ch = 4 * g + t
                 nc.vector.tensor_scalar(
                     out=cl[:, t, :],
-                    in0=xs[:, t, :],
+                    in0=xs_t[v][:, t, :],
                     scalar1=thr[:, 8 + ch : 9 + ch],
                     scalar2=thr[:, ch : ch + 1],
                     op0=ALU.max,
                     op1=ALU.min,
                 )
+            cl_t[v] = cl
+
+        def damp(v):
+            cl = cl_t[v]
+            kp = work.tile([P, 4, ROWS], BF16, name="kp")
+            h = work.tile([P, ROWS, 4], BF16, align_bytes=64, name="h")
             for b in range(2):
                 cols = slice(256 * b, 256 * b + 256)
-                bank = banks[(i, g, b)]
-                nc.vector.tensor_tensor(out=kp[:, :, cols], in0=cl[:, :, cols], in1=bank[:], op=ALU.is_equal)
+                nc.vector.tensor_tensor(out=kp[:, :, cols], in0=cl[:, :, cols], in1=banks[(v, b)][:], op=ALU.is_equal)
             for b in range(2):
                 cols = slice(256 * b, 256 * b + 256)
-                bank = banks[(i, g, b)]
                 nc.vector.scalar_tensor_tensor(
                     out=h[:, cols, :],
                     in0=kp[:, :, cols].rearrange("p t s -> p s t"),
                     scalar=0.01,
-                    in1=bank[:].rearrange("p t s -> p s t"),
+                    in1=banks[(v, b)][:].rearrange("p t s -> p s t"),
                     op0=ALU.max,
                     op1=ALU.mult,
                 )
+            h_t[v] = h
+
+        def quant(v):
+            i, g = divmod(v, G)
+            if g == 0:
+                codes = work.tile([P, G, ROWS], U32, align_bytes=64, name="codes")
+                scl = work.tile([P, G, ROWS], U8, align_bytes=64, name="scl")
+                codes_t[i] = codes
+                scl_t[i] = scl
             nc.vector.quantize_mx(
                 out=codes_t[i][:, g, :].bitcast(FP8X4),
                 scales=scl_t[i][:, g, :],
-                in_=h[:].rearrange("p s t -> p (s t)"),
+                in_=h_t[v][:].rearrange("p s t -> p (s t)"),
             )
 
+        def add_cur_vector(i, acc, j, hf):
+            cols = slice(512 * hf, 512 * hf + 512)
+            nc.vector.tensor_tensor(out=o_t[i][:, j, cols], in0=acc[:], in1=c_t[i][:, j, cols], op=ALU.add)
+
         def matmuls(i):
+            last = i == NST - 1
             ot = oout.tile([P, JT, SC], F32, name="ot")
             o_t[i] = ot
-            codes = codes_t[i]
-            scl = scl_t[i]
-            ct = c_t[i]
-            for j in range(JT):
-                act_cols = []
-                for hf in range(2):
-                    acc = accp.tile([P, 512], F32, name="acc")
-                    for g in range(G):
-                        nc.tensor.matmul_mx(
-                            out=acc[:],
-                            lhsT=codes[:, g, 128 * j : 128 * j + 128].bitcast(FP8X4),
-                            lhsT_scale=scl[:, g, 128 * j : 128 * j + 128],
-                            rhs=bcodes[:, g, 512 * hf : 512 * hf + 512].bitcast(FP8X4),
-                            rhs_scale=bscl[:, g, 512 * hf : 512 * hf + 512],
-                            start=(g == 0),
-                            stop=(g == G - 1),
-                        )
-                    cols = slice(512 * hf, 512 * hf + 512)
-                    if (j, hf) in DVE_BANKS or i == NST - 1:
-                        nc.vector.tensor_tensor(out=ot[:, j, cols], in0=acc[:], in1=ct[:, j, cols], op=ALU.add)
-                    else:
-                        nc.scalar.copy(out=ot[:, j, cols], in_=acc[:])
-                        act_cols.append(hf)
-                if len(act_cols) == 2:
-                    nc.gpsimd.tensor_tensor(out=ot[:, j, :], in0=ot[:, j, :], in1=ct[:, j, :], op=ALU.add)
-                elif len(act_cols) == 1:
-                    cols = slice(512 * act_cols[0], 512 * act_cols[0] + 512)
-                    nc.gpsimd.tensor_tensor(out=ot[:, j, cols], in0=ot[:, j, cols], in1=ct[:, j, cols], op=ALU.add)
-                if i == NST - 1:
-                    nc.sync.dma_start(out=ov[i][:, SC * j : SC * j + SC], in_=ot[:, j, :])
+            pend[i] = []
+            for n in range(2 * JT):
+                j, hf = divmod(n, 2)
+                acc = accp.tile([P, 512], F32, name="acc")
+                for g in range(G):
+                    nc.tensor.matmul_mx(
+                        out=acc[:],
+                        lhsT=codes_t[i][:, g, 128 * j : 128 * j + 128].bitcast(FP8X4),
+                        lhsT_scale=scl_t[i][:, g, 128 * j : 128 * j + 128],
+                        rhs=bcodes[:, g, 512 * hf : 512 * hf + 512].bitcast(FP8X4),
+                        rhs_scale=bscl[:, g, 512 * hf : 512 * hf + 512],
+                        start=(g == 0),
+                        stop=(g == G - 1),
+                    )
+                cols = slice(512 * hf, 512 * hf + 512)
+                if last:
+                    add_cur_vector(i, acc, j, hf)
+                    if hf == 1:
+                        nc.sync.dma_start(out=ov[i][:, SC * j : SC * j + SC], in_=ot[:, j, :])
+                elif n in DVE_BANKS:
+                    pend[i].append((n, acc, j, hf))
+                else:
+                    nc.scalar.copy(out=ot[:, j, cols], in_=acc[:])
+                    nc.gpsimd.tensor_tensor(out=ot[:, j, cols], in0=ot[:, j, cols], in1=c_t[i][:, j, cols], op=ALU.add)
+
+        def vector_banks(i, lo_n, hi_n):
+            for n, acc, j, hf in pend[i]:
+                if lo_n <= n < hi_n:
+                    add_cur_vector(i, acc, j, hf)
 
         def store(i):
-            if i < NST - 1:
-                nc.sync.dma_start(out=ov[i], in_=o_t[i][:].rearrange("p j n -> p (j n)"))
+            nc.sync.dma_start(out=ov[i], in_=o_t[i][:].rearrange("p j n -> p (j n)"))
 
-        regroup_b(0, "v")
-        quant_b(0)
-        transposes(0, 0)
-        copies(0, 0)
-        transposes(0, 1)
-        copies(0, 1)
-        regroup_b(1, "s")
-        masks(0, 0)
-        quant_b(1)
-        masks(0, 1)
+        nc.sync.dma_start(out=vt[0:8, :], in_=avail_bundle.rearrange("(c p) -> c p", p=P))
+        nc.sync.dma_start(out=vt[8:16, :], in_=alloc_bundle.rearrange("(c p) -> c p", p=P))
+        load_x(0, pieces=2)
+        load_b(0)
+        load_b(1)
+        load_x(1)
+        load_c(0)
+        load_x(2)
+        load_c(1)
 
-        for i in range(NST):
-            if i + 2 < NST:
-                load_x(i + 2)
-                load_c(i + 2)
-            if i + 1 < NST:
-                transposes(i + 1, 0)
-                copies(i + 1, 0)
-                transposes(i + 1, 1)
-                copies(i + 1, 1)
-            matmuls(i)
-            if i + 1 < NST:
-                masks(i + 1, 0)
-                masks(i + 1, 1)
-            store(i)
+        thr_ps = xtp.tile([P, P], BF16, tag="xt", name="thr_ps")
+        nc.tensor.transpose(thr_ps[:], vt[:], ident[:])
+        nc.vector.tensor_scalar(out=thr[:, 0:8], in0=thr_ps[:, 0:8], scalar1=0.0, scalar2=None, op0=ALU.max)
+        nc.vector.tensor_scalar(
+            out=thr[:, 8:16], in0=thr_ps[:, 8:16], scalar1=-1.0, scalar2=0.0, op0=ALU.mult, op1=ALU.min
+        )
+        transposes(0)
+        copies(0)
+        transposes(1)
+        copies(1)
+        regroup_b(0, "s")
+        regroup_b(1, "g")
+
+        for v in range(NU):
+            m = v // 2
+            even = v % 2 == 0
+            if even:
+                if m >= 2:
+                    store(m - 2)
+                if m + 2 < NST:
+                    load_c(m + 2)
+                if m + 3 < NST:
+                    load_x(m + 3)
+            clamps(v)
+            if v >= 1:
+                quant(v - 1)
+            if v == 2:
+                quant_b(0)
+                quant_b(1)
+            if even and m >= 1:
+                matmuls(m - 1)
+            if not even and m >= 1:
+                vector_banks(m - 1, 4, 8)
+            damp(v)
+            if v + 2 < NU:
+                transposes(v + 2)
+                copies(v + 2)
+            if even and m >= 1:
+                vector_banks(m - 1, 0, 4)
+        quant(NU - 1)
+        store(NST - 2)
+        matmuls(NST - 1)

@@ -20,15 +20,22 @@ NST = S // ROWS
 G = B // 512
 NU = NST * G
 PIN = True
-DVE_BANKS = (3, 7)
+VEC_EVERY = 2
 
 
 def tile_optblockv2_t_kernel(tc, proba, cur_inven, bun_sc, avail_bundle, alloc_bundle, out):
     nc = tc.nc
-    xv = proba.rearrange("(i r q) -> i r q", r=P, q=JT * B)
+    xv = proba.rearrange("(i r j k) -> i r j k", r=P, j=JT, k=B)
     cv = cur_inven.rearrange("(i r j) n -> i r (j n)", r=P, j=JT)
     ov = out.rearrange("o (i r q) -> (o i) r q", r=P, q=JT * SC)
     bv = bun_sc.rearrange("(g t p) n -> g p t n", t=4, p=P)
+
+    units = []
+    for i in range(NST - 1):
+        for g in range(G):
+            units.append([(i, g, 0), (i, g, 1)])
+    for b in range(2):
+        units.append([(NST - 1, 0, b), (NST - 1, 1, b)])
 
     with ExitStack() as ctx:
         const = ctx.enter_context(tc.tile_pool(name="const", bufs=1))
@@ -48,10 +55,8 @@ def tile_optblockv2_t_kernel(tc, proba, cur_inven, bun_sc, avail_bundle, alloc_b
         xs_t = {}
         cl_t = {}
         h_t = {}
-        codes_t = {}
-        scl_t = {}
+        words = {}
         bgrp = {}
-        pend = {}
 
         ident = const.tile([P, P], BF16)
         make_identity(nc, ident[:])
@@ -65,12 +70,13 @@ def tile_optblockv2_t_kernel(tc, proba, cur_inven, bun_sc, avail_bundle, alloc_b
         def load_b(g):
             nc.sync.dma_start(out=braw[:, 4 * g : 4 * g + 4, :], in_=bv[g])
 
-        def load_x(i, pieces=1):
+        def load_x(i, by_pass=False):
             xt = xin.tile([P, JT, B], BF16, name="xt")
-            w = JT * B // pieces
-            flat = xt[:].rearrange("p j k -> p (j k)")
-            for q in range(pieces):
-                nc.sync.dma_start(out=flat[:, w * q : w * q + w], in_=xv[i][:, w * q : w * q + w])
+            if by_pass:
+                for g in range(G):
+                    nc.sync.dma_start(out=xt[:, :, 512 * g : 512 * g + 512], in_=xv[i][:, :, 512 * g : 512 * g + 512])
+            else:
+                nc.sync.dma_start(out=xt[:], in_=xv[i])
             x_t[i] = xt
 
         def load_c(i):
@@ -98,8 +104,7 @@ def tile_optblockv2_t_kernel(tc, proba, cur_inven, bun_sc, avail_bundle, alloc_b
             )
 
         def transposes(v):
-            i, g = divmod(v, G)
-            for b in range(2):
+            for a, (i, g, b) in enumerate(units[v]):
                 bank = xtp.tile([P, 4, 256], BF16, tag="xt", name="bank")
                 for t in range(4):
                     for jj in range(2):
@@ -107,105 +112,112 @@ def tile_optblockv2_t_kernel(tc, proba, cur_inven, bun_sc, avail_bundle, alloc_b
                         nc.tensor.transpose(
                             bank[:, t, 128 * jj : 128 * jj + 128], x_t[i][:, 2 * b + jj, k0 : k0 + 128], ident[:]
                         )
-                banks[(v, b)] = bank
+                banks[(v, a)] = bank
 
         def copies(v):
-            xs = work.tile([P, 4, ROWS], BF16, name="xs", bufs=3)
-            for b in range(2):
-                nc.scalar.copy(out=xs[:, :, 256 * b : 256 * b + 256], in_=banks[(v, b)][:])
+            xs = work.tile([P, 2, 4, 256], BF16, name="xs", bufs=3)
+            for a in range(2):
+                nc.scalar.copy(out=xs[:, a, :, :], in_=banks[(v, a)][:])
             xs_t[v] = xs
 
+        def clamp(dst, src, ch):
+            nc.vector.tensor_scalar(
+                out=dst,
+                in0=src,
+                scalar1=thr[:, 8 + ch : 9 + ch],
+                scalar2=thr[:, ch : ch + 1],
+                op0=ALU.max,
+                op1=ALU.min,
+            )
+
         def clamps(v):
-            g = v % G
-            cl = work.tile([P, 4, ROWS], BF16, name="cl")
+            cl = work.tile([P, 2, 4, 256], BF16, name="cl")
+            xs = xs_t[v]
+            g0 = units[v][0][1]
+            g1 = units[v][1][1]
             for t in range(4):
-                ch = 4 * g + t
-                nc.vector.tensor_scalar(
-                    out=cl[:, t, :],
-                    in0=xs_t[v][:, t, :],
-                    scalar1=thr[:, 8 + ch : 9 + ch],
-                    scalar2=thr[:, ch : ch + 1],
-                    op0=ALU.max,
-                    op1=ALU.min,
-                )
+                if g0 == g1:
+                    clamp(cl[:, :, t, :], xs[:, :, t, :], 4 * g0 + t)
+                else:
+                    clamp(cl[:, 0, t, :], xs[:, 0, t, :], 4 * g0 + t)
+                    clamp(cl[:, 1, t, :], xs[:, 1, t, :], 4 * g1 + t)
             cl_t[v] = cl
 
         def damp(v):
             cl = cl_t[v]
-            kp = work.tile([P, 4, ROWS], BF16, name="kp")
-            h = work.tile([P, ROWS, 4], BF16, align_bytes=64, name="h")
-            for b in range(2):
-                cols = slice(256 * b, 256 * b + 256)
-                nc.vector.tensor_tensor(out=kp[:, :, cols], in0=cl[:, :, cols], in1=banks[(v, b)][:], op=ALU.is_equal)
-            for b in range(2):
-                cols = slice(256 * b, 256 * b + 256)
+            kp = work.tile([P, 2, 4, 256], BF16, name="kp")
+            h = work.tile([P, 2, 256, 4], BF16, align_bytes=64, name="h")
+            for a in range(2):
+                nc.vector.tensor_tensor(out=kp[:, a, :, :], in0=cl[:, a, :, :], in1=banks[(v, a)][:], op=ALU.is_equal)
+            for a in range(2):
                 nc.vector.scalar_tensor_tensor(
-                    out=h[:, cols, :],
-                    in0=kp[:, :, cols].rearrange("p t s -> p s t"),
+                    out=h[:, a, :, :],
+                    in0=kp[:, a, :, :].rearrange("p t s -> p s t"),
                     scalar=0.01,
-                    in1=banks[(v, b)][:].rearrange("p t s -> p s t"),
+                    in1=banks[(v, a)][:].rearrange("p t s -> p s t"),
                     op0=ALU.max,
                     op1=ALU.mult,
                 )
             h_t[v] = h
 
         def quant(v):
-            i, g = divmod(v, G)
-            if g == 0:
-                codes = work.tile([P, G, ROWS], U32, align_bytes=64, name="codes")
-                scl = work.tile([P, G, ROWS], U8, align_bytes=64, name="scl")
-                codes_t[i] = codes
-                scl_t[i] = scl
+            codes = work.tile([P, 2, 256], U32, align_bytes=64, name="codes", bufs=5)
+            scl = work.tile([P, 2, 256], U8, align_bytes=64, name="scl", bufs=5)
             nc.vector.quantize_mx(
-                out=codes_t[i][:, g, :].bitcast(FP8X4),
-                scales=scl_t[i][:, g, :],
-                in_=h_t[v][:].rearrange("p s t -> p (s t)"),
+                out=codes[:].rearrange("p a s -> p (a s)").bitcast(FP8X4),
+                scales=scl[:].rearrange("p a s -> p (a s)"),
+                in_=h_t[v][:].rearrange("p a s t -> p (a s t)"),
             )
+            for a, key in enumerate(units[v]):
+                words[key] = (codes[:, a, :], scl[:, a, :])
 
         def add_cur_vector(i, acc, j, hf):
             cols = slice(512 * hf, 512 * hf + 512)
             nc.vector.tensor_tensor(out=o_t[i][:, j, cols], in0=acc[:], in1=c_t[i][:, j, cols], op=ALU.add)
 
-        def matmuls(i):
-            last = i == NST - 1
-            ot = oout.tile([P, JT, SC], F32, name="ot")
-            o_t[i] = ot
-            pend[i] = []
-            for n in range(2 * JT):
-                j, hf = divmod(n, 2)
+        def job(i, b, vec_later=(), vec_now=False):
+            if b == 0:
+                ot = oout.tile([P, JT, SC], F32, name="ot")
+                o_t[i] = ot
+            later = []
+            for n in range(4):
+                jj, hf = divmod(n, 2)
+                j = 2 * b + jj
                 acc = accp.tile([P, 512], F32, name="acc")
                 for g in range(G):
+                    cw, sw = words[(i, g, b)]
                     nc.tensor.matmul_mx(
                         out=acc[:],
-                        lhsT=codes_t[i][:, g, 128 * j : 128 * j + 128].bitcast(FP8X4),
-                        lhsT_scale=scl_t[i][:, g, 128 * j : 128 * j + 128],
+                        lhsT=cw[:, 128 * jj : 128 * jj + 128].bitcast(FP8X4),
+                        lhsT_scale=sw[:, 128 * jj : 128 * jj + 128],
                         rhs=bcodes[:, g, 512 * hf : 512 * hf + 512].bitcast(FP8X4),
                         rhs_scale=bscl[:, g, 512 * hf : 512 * hf + 512],
                         start=(g == 0),
                         stop=(g == G - 1),
                     )
                 cols = slice(512 * hf, 512 * hf + 512)
-                if last:
+                if vec_now:
                     add_cur_vector(i, acc, j, hf)
                     if hf == 1:
-                        nc.sync.dma_start(out=ov[i][:, SC * j : SC * j + SC], in_=ot[:, j, :])
-                elif n in DVE_BANKS:
-                    pend[i].append((n, acc, j, hf))
+                        nc.sync.dma_start(out=ov[i][:, SC * j : SC * j + SC], in_=o_t[i][:, j, :])
+                elif n in vec_later:
+                    later.append((i, acc, j, hf))
                 else:
-                    nc.scalar.copy(out=ot[:, j, cols], in_=acc[:])
-                    nc.gpsimd.tensor_tensor(out=ot[:, j, cols], in0=ot[:, j, cols], in1=c_t[i][:, j, cols], op=ALU.add)
+                    nc.scalar.copy(out=o_t[i][:, j, cols], in_=acc[:])
+                    nc.gpsimd.tensor_tensor(
+                        out=o_t[i][:, j, cols], in0=o_t[i][:, j, cols], in1=c_t[i][:, j, cols], op=ALU.add
+                    )
+            return later
 
-        def vector_banks(i, lo_n, hi_n):
-            for n, acc, j, hf in pend[i]:
-                if lo_n <= n < hi_n:
-                    add_cur_vector(i, acc, j, hf)
-
-        def store(i):
-            nc.sync.dma_start(out=ov[i], in_=o_t[i][:].rearrange("p j n -> p (j n)"))
+        def store(i, b):
+            w = 2 * SC
+            nc.sync.dma_start(
+                out=ov[i][:, w * b : w * b + w], in_=o_t[i][:, 2 * b : 2 * b + 2, :].rearrange("p j n -> p (j n)")
+            )
 
         nc.sync.dma_start(out=vt[0:8, :], in_=avail_bundle.rearrange("(c p) -> c p", p=P))
         nc.sync.dma_start(out=vt[8:16, :], in_=alloc_bundle.rearrange("(c p) -> c p", p=P))
-        load_x(0, pieces=2)
+        load_x(0, by_pass=True)
         load_b(0)
         load_b(1)
         load_x(1)
@@ -226,12 +238,19 @@ def tile_optblockv2_t_kernel(tc, proba, cur_inven, bun_sc, avail_bundle, alloc_b
         regroup_b(0, "s")
         regroup_b(1, "g")
 
+        jobs_at = {}
+        for i in range(NST - 1):
+            jobs_at[2 * i + 2] = [(i, 0)]
+            jobs_at[2 * i + 3] = [(i, 1)]
+        jobs_at[NU - 1].append((NST - 1, 0))
+
+        count = 0
+        held = []
         for v in range(NU):
             m = v // 2
-            even = v % 2 == 0
-            if even:
-                if m >= 2:
-                    store(m - 2)
+            for i, b in jobs_at.get(v - 2, []):
+                store(i, b)
+            if v % 2 == 0:
                 if m + 2 < NST:
                     load_c(m + 2)
                 if m + 3 < NST:
@@ -242,16 +261,24 @@ def tile_optblockv2_t_kernel(tc, proba, cur_inven, bun_sc, avail_bundle, alloc_b
             if v == 2:
                 quant_b(0)
                 quant_b(1)
-            if even and m >= 1:
-                matmuls(m - 1)
-            if not even and m >= 1:
-                vector_banks(m - 1, 4, 8)
+            later = []
+            for i, b in jobs_at.get(v, []):
+                if i == NST - 1:
+                    held.extend(job(i, b, vec_later=(2, 3)))
+                else:
+                    count += 1
+                    take = VEC_EVERY > 0 and count % VEC_EVERY == 0
+                    later.extend(job(i, b, vec_later=(3,) if take else ()))
             damp(v)
             if v + 2 < NU:
                 transposes(v + 2)
                 copies(v + 2)
-            if even and m >= 1:
-                vector_banks(m - 1, 0, 4)
+            for i, acc, j, hf in later:
+                add_cur_vector(i, acc, j, hf)
         quant(NU - 1)
-        store(NST - 2)
-        matmuls(NST - 1)
+        for i, acc, j, hf in held:
+            add_cur_vector(i, acc, j, hf)
+        store(NST - 2, 0)
+        store(NST - 2, 1)
+        store(NST - 1, 0)
+        job(NST - 1, 1, vec_now=True)

@@ -20,7 +20,7 @@ NST = S // ROWS
 G = B // 512
 NU = NST * G
 PIN = True
-VEC_EVERY = 2
+VEC_EVERY = 0
 
 
 def tile_optblockv2_t_kernel(tc, proba, cur_inven, bun_sc, avail_bundle, alloc_bundle, out):

@@ -20,7 +20,7 @@ NST = S // ROWS
 G = B // 512
 NU = NST * G
 PIN = True
-VEC_EVERY = 0
+VEC_EVERY = 1
 
 
 def tile_optblockv2_t_kernel(tc, proba, cur_inven, bun_sc, avail_bundle, alloc_bundle, out):
@@ -73,8 +73,9 @@ def tile_optblockv2_t_kernel(tc, proba, cur_inven, bun_sc, avail_bundle, alloc_b
         def load_x(i, by_pass=False):
             xt = xin.tile([P, JT, B], BF16, name="xt")
             if by_pass:
-                for g in range(G):
-                    nc.sync.dma_start(out=xt[:, :, 512 * g : 512 * g + 512], in_=xv[i][:, :, 512 * g : 512 * g + 512])
+                nc.sync.dma_start(out=xt[:, 0:2, 0:512], in_=xv[i][:, 0:2, 0:512])
+                nc.sync.dma_start(out=xt[:, 2:4, 0:512], in_=xv[i][:, 2:4, 0:512])
+                nc.sync.dma_start(out=xt[:, :, 512:1024], in_=xv[i][:, :, 512:1024])
             else:
                 nc.sync.dma_start(out=xt[:], in_=xv[i])
             x_t[i] = xt
@@ -135,12 +136,13 @@ def tile_optblockv2_t_kernel(tc, proba, cur_inven, bun_sc, avail_bundle, alloc_b
             xs = xs_t[v]
             g0 = units[v][0][1]
             g1 = units[v][1][1]
-            for t in range(4):
-                if g0 == g1:
+            if g0 == g1 and v > 0:
+                for t in range(4):
                     clamp(cl[:, :, t, :], xs[:, :, t, :], 4 * g0 + t)
-                else:
-                    clamp(cl[:, 0, t, :], xs[:, 0, t, :], 4 * g0 + t)
-                    clamp(cl[:, 1, t, :], xs[:, 1, t, :], 4 * g1 + t)
+            else:
+                for a, ga in enumerate((g0, g1)):
+                    for t in range(4):
+                        clamp(cl[:, a, t, :], xs[:, a, t, :], 4 * ga + t)
             cl_t[v] = cl
 
         def damp(v):

@@ -269,7 +269,7 @@ def tile_optblockv2_t_kernel(tc, proba, cur_inven, bun_sc, avail_bundle, alloc_b
                     held.extend(job(i, b, vec_later=(2, 3)))
                 else:
                     count += 1
-                    take = VEC_EVERY > 0 and count % VEC_EVERY == 0
+                    take = count % 4 != 0
                     later.extend(job(i, b, vec_later=(3,) if take else ()))
             damp(v)
             if v + 2 < NU:

from contextlib import ExitStack

import concourse.mybir as mybir
from concourse.masks import make_identity

FP8X4 = mybir.dt.float8_e4m3fn_x4
BF16 = mybir.dt.bfloat16
F32 = mybir.dt.float32
U32 = mybir.dt.uint32
U8 = mybir.dt.uint8
ALU = mybir.AluOpType

S, B, SC = 4096, 1024, 1024
FLOPS = 2 * S * B * SC

P = 128
JT = 4
ROWS = P * JT
NST = S // ROWS
G = B // 512
NU = NST * G
PIN = True
VEC_EVERY = 1


def tile_optblockv2_t_kernel(tc, proba, cur_inven, bun_sc, avail_bundle, alloc_bundle, out):
    nc = tc.nc
    xv = proba.rearrange("(i r j k) -> i r j k", r=P, j=JT, k=B)
    cv = cur_inven.rearrange("(i r j) n -> i r (j n)", r=P, j=JT)
    ov = out.rearrange("o (i r q) -> (o i) r q", r=P, q=JT * SC)
    bv = bun_sc.rearrange("(g t p) n -> g p t n", t=4, p=P)

    units = []
    for i in range(NST - 1):
        for g in range(G):
            units.append([(i, g, 0), (i, g, 1)])
    for b in range(2):
        units.append([(NST - 1, 0, b), (NST - 1, 1, b)])

    with ExitStack() as ctx:
        const = ctx.enter_context(tc.tile_pool(name="const", bufs=1))
        xin = ctx.enter_context(tc.tile_pool(name="xin", bufs=3))
        cin = ctx.enter_context(tc.tile_pool(name="cin", bufs=4))
        oout = ctx.enter_context(tc.tile_pool(name="oout", bufs=3))
        work = ctx.enter_context(tc.tile_pool(name="work", bufs=2))
        xtp = ctx.enter_context(tc.psum_pool(name="xtp", bufs=4))
        accp = ctx.enter_context(tc.psum_pool(name="accp", bufs=4))
        if PIN:
            ctx.enter_context(tc.manual_schedule())

        x_t = {}
        c_t = {}
        o_t = {}
        banks = {}
        xs_t = {}
        cl_t = {}
        h_t = {}
        words = {}
        bgrp = {}

        ident = const.tile([P, P], BF16)
        make_identity(nc, ident[:])
        vt = const.tile([P, P], BF16)
        nc.vector.memset(vt[:], 0.0)
        braw = const.tile([P, 2 * 4, SC], BF16)
        bcodes = const.tile([P, G, SC], U32, align_bytes=64)
        bscl = const.tile([P, G, SC], U8, align_bytes=64)
        thr = const.tile([P, 16], F32)

        def load_b(g):
            nc.sync.dma_start(out=braw[:, 4 * g : 4 * g + 4, :], in_=bv[g])

        def load_x(i, by_pass=False):
            xt = xin.tile([P, JT, B], BF16, name="xt")
            if by_pass:
                nc.sync.dma_start(out=xt[:, 0:2, 0:512], in_=xv[i][:, 0:2, 0:512])
                nc.sync.dma_start(out=xt[:, 2:4, 0:512], in_=xv[i][:, 2:4, 0:512])
                nc.sync.dma_start(out=xt[:, :, 512:1024], in_=xv[i][:, :, 512:1024])
            else:
                nc.sync.dma_start(out=xt[:], in_=xv[i])
            x_t[i] = xt

        def load_c(i):
            ct = cin.tile([P, JT, SC], BF16, name="ct")
            nc.sync.dma_start(out=ct[:].rearrange("p j n -> p (j n)"), in_=cv[i])
            c_t[i] = ct

        def regroup_b(g, eng):
            bg = const.tile([P, SC, 4], BF16, align_bytes=64, name="bgrp%d" % g)
            dst = bg[:].rearrange("p (c i) t -> p c t i", i=4)
            src = braw[:, 4 * g : 4 * g + 4, :].rearrange("p t (c i) -> p c t i", i=4)
            if eng == "v":
                nc.vector.tensor_copy(out=dst, in_=src)
            elif eng == "s":
                nc.scalar.copy(out=dst, in_=src)
            else:
                nc.gpsimd.tensor_scalar(out=dst, in0=src, scalar1=1.0, scalar2=0.0, op0=ALU.mult, op1=ALU.add)
            bgrp[g] = bg

        def quant_b(g):
            nc.vector.quantize_mx(
                out=bcodes[:, g, :].bitcast(FP8X4),
                scales=bscl[:, g, :],
                in_=bgrp[g][:].rearrange("p n t -> p (n t)"),
            )

        def transposes(v):
            for a, (i, g, b) in enumerate(units[v]):
                bank = xtp.tile([P, 4, 256], BF16, tag="xt", name="bank")
                for t in range(4):
                    for jj in range(2):
                        k0 = 512 * g + 128 * t
                        nc.tensor.transpose(
                            bank[:, t, 128 * jj : 128 * jj + 128], x_t[i][:, 2 * b + jj, k0 : k0 + 128], ident[:]
                        )
                banks[(v, a)] = bank

        def copies(v):
            xs = work.tile([P, 2, 4, 256], BF16, name="xs", bufs=3)
            for a in range(2):
                nc.scalar.copy(out=xs[:, a, :, :], in_=banks[(v, a)][:])
            xs_t[v] = xs

        def clamp(dst, src, ch):
            nc.vector.tensor_scalar(
                out=dst,
                in0=src,
                scalar1=thr[:, 8 + ch : 9 + ch],
                scalar2=thr[:, ch : ch + 1],
                op0=ALU.max,
                op1=ALU.min,
            )

        def clamps(v):
            cl = work.tile([P, 2, 4, 256], BF16, name="cl")
            xs = xs_t[v]
            g0 = units[v][0][1]
            g1 = units[v][1][1]
            if g0 == g1 and v > 0:
                for t in range(4):
                    clamp(cl[:, :, t, :], xs[:, :, t, :], 4 * g0 + t)
            else:
                for a, ga in enumerate((g0, g1)):
                    for t in range(4):
                        clamp(cl[:, a, t, :], xs[:, a, t, :], 4 * ga + t)
            cl_t[v] = cl

        def damp(v):
            cl = cl_t[v]
            kp = work.tile([P, 2, 4, 256], BF16, name="kp")
            h = work.tile([P, 2, 256, 4], BF16, align_bytes=64, name="h")
            for a in range(2):
                nc.vector.tensor_tensor(out=kp[:, a, :, :], in0=cl[:, a, :, :], in1=banks[(v, a)][:], op=ALU.is_equal)
            for a in range(2):
                nc.vector.scalar_tensor_tensor(
                    out=h[:, a, :, :],
                    in0=kp[:, a, :, :].rearrange("p t s -> p s t"),
                    scalar=0.01,
                    in1=banks[(v, a)][:].rearrange("p t s -> p s t"),
                    op0=ALU.max,
                    op1=ALU.mult,
                )
            h_t[v] = h

        def quant(v):
            codes = work.tile([P, 2, 256], U32, align_bytes=64, name="codes", bufs=5)
            scl = work.tile([P, 2, 256], U8, align_bytes=64, name="scl", bufs=5)
            nc.vector.quantize_mx(
                out=codes[:].rearrange("p a s -> p (a s)").bitcast(FP8X4),
                scales=scl[:].rearrange("p a s -> p (a s)"),
                in_=h_t[v][:].rearrange("p a s t -> p (a s t)"),
            )
            for a, key in enumerate(units[v]):
                words[key] = (codes[:, a, :], scl[:, a, :])

        def add_cur_vector(i, acc, j, hf):
            cols = slice(512 * hf, 512 * hf + 512)
            nc.vector.tensor_tensor(out=o_t[i][:, j, cols], in0=acc[:], in1=c_t[i][:, j, cols], op=ALU.add)

        def job(i, b, vec_later=(), vec_now=False):
            if b == 0:
                ot = oout.tile([P, JT, SC], F32, name="ot")
                o_t[i] = ot
            later = []
            for n in range(4):
                jj, hf = divmod(n, 2)
                j = 2 * b + jj
                acc = accp.tile([P, 512], F32, name="acc")
                for g in range(G):
                    cw, sw = words[(i, g, b)]
                    nc.tensor.matmul_mx(
                        out=acc[:],
                        lhsT=cw[:, 128 * jj : 128 * jj + 128].bitcast(FP8X4),
                        lhsT_scale=sw[:, 128 * jj : 128 * jj + 128],
                        rhs=bcodes[:, g, 512 * hf : 512 * hf + 512].bitcast(FP8X4),
                        rhs_scale=bscl[:, g, 512 * hf : 512 * hf + 512],
                        start=(g == 0),
                        stop=(g == G - 1),
                    )
                cols = slice(512 * hf, 512 * hf + 512)
                if vec_now:
                    add_cur_vector(i, acc, j, hf)
                    if hf == 1:
                        nc.sync.dma_start(out=ov[i][:, SC * j : SC * j + SC], in_=o_t[i][:, j, :])
                elif n in vec_later:
                    later.append((i, acc, j, hf))
                else:
                    nc.scalar.copy(out=o_t[i][:, j, cols], in_=acc[:])
                    nc.gpsimd.tensor_tensor(
                        out=o_t[i][:, j, cols], in0=o_t[i][:, j, cols], in1=c_t[i][:, j, cols], op=ALU.add
                    )
            return later

        def store(i, b):
            w = 2 * SC
            nc.sync.dma_start(
                out=ov[i][:, w * b : w * b + w], in_=o_t[i][:, 2 * b : 2 * b + 2, :].rearrange("p j n -> p (j n)")
            )

        nc.sync.dma_start(out=vt[0:8, :], in_=avail_bundle.rearrange("(c p) -> c p", p=P))
        nc.sync.dma_start(out=vt[8:16, :], in_=alloc_bundle.rearrange("(c p) -> c p", p=P))
        load_x(0, by_pass=True)
        load_b(0)
        load_b(1)
        load_x(1)
        load_c(0)
        load_x(2)
        load_c(1)

        thr_ps = xtp.tile([P, P], BF16, tag="xt", name="thr_ps")
        nc.tensor.transpose(thr_ps[:], vt[:], ident[:])
        nc.vector.tensor_scalar(out=thr[:, 0:8], in0=thr_ps[:, 0:8], scalar1=0.0, scalar2=None, op0=ALU.max)
        nc.vector.tensor_scalar(
            out=thr[:, 8:16], in0=thr_ps[:, 8:16], scalar1=-1.0, scalar2=0.0, op0=ALU.mult, op1=ALU.min
        )
        transposes(0)
        copies(0)
        transposes(1)
        copies(1)
        regroup_b(0, "s")
        regroup_b(1, "g")

        jobs_at = {}
        for i in range(NST - 1):
            jobs_at[2 * i + 2] = [(i, 0)]
            jobs_at[2 * i + 3] = [(i, 1)]
        jobs_at[NU - 1].append((NST - 1, 0))

        count = 0
        held = []
        for v in range(NU):
            m = v // 2
            for i, b in jobs_at.get(v - 2, []):
                store(i, b)
            if v % 2 == 0:
                if m + 2 < NST:
                    load_c(m + 2)
                if m + 3 < NST:
                    load_x(m + 3)
            clamps(v)
            if v >= 1:
                quant(v - 1)
            if v == 2:
                quant_b(0)
                quant_b(1)
            later = []
            for i, b in jobs_at.get(v, []):
                if i == NST - 1:
                    held.extend(job(i, b, vec_later=(2, 3)))
                else:
                    count += 1
                    take = count % 4 != 0
                    later.extend(job(i, b, vec_later=(3,) if take else ()))
            damp(v)
            if v + 2 < NU:
                transposes(v + 2)
                copies(v + 2)
            for i, acc, j, hf in later:
                add_cur_vector(i, acc, j, hf)
        quant(NU - 1)
        for i, acc, j, hf in held:
            add_cur_vector(i, acc, j, hf)
        store(NST - 2, 0)
        store(NST - 2, 1)
        store(NST - 1, 0)
        job(NST - 1, 1, vec_now=True)
